import numpy as np
import ml_dtypes


BF16 = ml_dtypes.bfloat16


def bf(x):
    return np.asarray(x, np.float32).astype(BF16)


def f64(x):
    return np.asarray(x).astype(np.float64)


E2M1 = np.array([0.0, 0.5, 1.0, 1.5, 2.0, 3.0, 4.0, 6.0, -0.0, -0.5, -1.0, -1.5, -2.0, -3.0, -4.0, -6.0])


def pack_weight(w, fmt):
    k, n = w.shape
    w = f64(bf(w)).reshape(k // 32, 32, n)
    amax = np.abs(w).max(1)
    if fmt == "e4m3":
        byte = np.frexp(amax)[1] - 1 + 127 - 7
    else:
        mant, ex = np.frexp(amax / 6.0)
        byte = np.where(mant > 0.5, ex, ex - 1) + 127
    byte = np.clip(np.where(amax > 0, byte, 1), 1, 254)
    scaled = (w * np.exp2(127.0 - byte)[:, None, :]).reshape(k, n).astype(np.float32)
    by_word = np.ascontiguousarray(scaled.reshape(k // 512, 128, 4, n).transpose(0, 1, 3, 2))
    if fmt == "e4m3":
        words = by_word.astype(ml_dtypes.float8_e4m3fn).view(np.uint8)
    else:
        c = by_word.astype(ml_dtypes.float4_e2m1fn).view(np.uint8) & 0xF
        words = c[..., 0::2] | (c[..., 1::2] << 4)
    return np.ascontiguousarray(words), np.ascontiguousarray(byte.astype(np.uint8).reshape(k // 512, 16, n))


def unpack_weight(words, scales, fmt):
    g, p, n, _ = words.shape
    if fmt == "e4m3":
        vals = np.ascontiguousarray(words).view(ml_dtypes.float8_e4m3fn).astype(np.float64)
    else:
        nib = np.empty((g, p, n, 4), np.uint8)
        nib[..., 0::2] = words & 0xF
        nib[..., 1::2] = words >> 4
        vals = E2M1[nib]
    vals = vals * np.repeat(np.exp2(scales.astype(np.float64) - 127.0), 8, axis=1)[..., None]
    return vals.transpose(0, 1, 3, 2).reshape(g * 512, n)

def pack4(w):
    words, scales = pack_weight(w, "e2m1")
    return words.reshape(words.shape[0], 128, -1), scales


def unpack4(words, scales):
    return unpack_weight(words.reshape(words.shape[0], 128, -1, 2), scales, "e2m1")


def kspread(k):
    return np.exp2(np.repeat(np.random.randint(-6, 7, k // 32), 32).astype(np.float64))


B, S, D, NH, NKV, HD = 2, 1536, 2048, 16, 4, 128
EPS = 1e-6
QS = NH * HD
KS = NKV * HD
E = QS + KS + KS
HP = HD // 2


def rmsnorm(v, w):
    ms = np.mean(np.square(v), axis=-1, keepdims=True)
    return v * (1.0 / np.sqrt(ms + EPS)) * w


def apply_rotary_emb(v, fc):
    vs = v.reshape(*v.shape[:-1], HP, 2)
    f = fc[None, :, None, :, :]
    vr, vi = vs[..., 0], vs[..., 1]
    fr, fi = f[..., 0], f[..., 1]
    return np.stack([vr * fr - vi * fi, vi * fr + vr * fi], axis=-1).reshape(v.shape)


def setup_inputs():
    s = kspread(D)
    x = np.random.standard_normal((B, S, D)) * s
    x_words, x_scales = pack4(np.ascontiguousarray(x.reshape(B * S, D).T))
    freqs_cis = bf(np.random.standard_normal((S, HP, 2)))
    wqkv = np.random.standard_normal((E, D)) / np.sqrt(D) / s[None, :]
    words, scales = pack4(np.ascontiguousarray(wqkv.T))
    q_norm_w = bf(1.0 + 0.1 * np.random.standard_normal(HD))
    k_norm_w = bf(1.0 + 0.1 * np.random.standard_normal(HD))
    return {"x_words": x_words,
            "x_scales": x_scales,
            "freqs_cis": freqs_cis,
            "wqkv_words": words,
            "wqkv_scales": scales,
            "q_norm_w": q_norm_w,
            "k_norm_w": k_norm_w}


def reference(x_words, x_scales, freqs_cis, wqkv_words, wqkv_scales, q_norm_w, k_norm_w):
    fc = f64(freqs_cis)
    x = unpack4(x_words, x_scales).T.reshape(B, S, D)
    qkv = x @ unpack4(wqkv_words, wqkv_scales)
    q = qkv[..., :QS].reshape(B, S, NH, HD)
    k = qkv[..., QS:QS + KS].reshape(B, S, NKV, HD)
    v = qkv[..., QS + KS:].reshape(B, S, NKV, HD)
    q = rmsnorm(q, f64(q_norm_w))
    k = rmsnorm(k, f64(k_norm_w))
    q_rot = apply_rotary_emb(q, fc)
    k_rot = apply_rotary_emb(k, fc)
    return q_rot, k_rot, v

@@ -1,0 +1,236 @@
+from contextlib import ExitStack
+
+import concourse.mybir as mybir
+
+F32 = mybir.dt.float32
+BF16 = mybir.dt.bfloat16
+U8 = mybir.dt.uint8
+I32 = mybir.dt.int32
+FP4X4 = mybir.dt.float4_e2m1fn_x4
+ACT = mybir.ActivationFunctionType
+ALU = mybir.AluOpType
+
+P = 128
+TOKENS = 3072
+D_IN = 2048
+PASSES = D_IN // 512
+HD = 128
+NBLK = 512
+HEADS_PER_BLK = NBLK // HD
+K_BLOCK = 4
+V_BLOCK = 5
+BLOCKS = 6
+TPG = 4
+GROUPS = TOKENS // (TPG * P)
+TOKEN_TILES = TOKENS // P
+POS_GROUPS = 3
+EPS = 1e-6
+INV_SQRT_HD = 1.0 / (128.0 ** 0.5)
+W_PLANE_RANGES = ((0, 1), (1, 3), (3, 6))
+X_PLANE_RANGES = ((0, 1), (1, 6))
+
+FLOPS = 2 * TOKENS * D_IN * 3072
+
+
+def tile_attention_pa_kernel(
+    tc, x_words, x_scales, freqs_cis, wqkv_words, wqkv_scales, q_norm_w, k_norm_w, out_0, out_1, out_2
+):
+    nc = tc.nc
+    with ExitStack() as ctx:
+        keep = ctx.enter_context(tc.tile_pool(name="keep", bufs=1))
+        work = ctx.enter_context(tc.tile_pool(name="work", bufs=4))
+        small = ctx.enter_context(tc.tile_pool(name="small", bufs=8))
+        psum = ctx.enter_context(tc.psum_pool(name="psum", bufs=8))
+
+        wq_b = keep.tile([P, HD], BF16, name="wq_b")
+        wk_b = keep.tile([P, HD], BF16, name="wk_b")
+        fc = keep.tile([P, 12, HD], BF16, name="fc")
+        fc_view = freqs_cis.rearrange("(t p) j e -> p t (j e)", p=P)
+        nc.gpsimd.dma_start(out=wq_b[:], in_=q_norm_w.partition_broadcast(P))
+        nc.gpsimd.dma_start(out=fc[:, 0:4, :], in_=fc_view[:, 0:4, :])
+        nc.gpsimd.dma_start(out=wk_b[:], in_=k_norm_w.partition_broadcast(P))
+        nc.gpsimd.dma_start(out=fc[:, 4:12, :], in_=fc_view[:, 4:12, :])
+
+        xc = []
+        wc = []
+        for c in range(GROUPS):
+            xc_t = keep.tile([P, PASSES, 2 * NBLK], U8, name="xc%d" % c, align_bytes=64)
+            xc.append(xc_t)
+        for n in range(BLOCKS):
+            wc_t = keep.tile([P, PASSES, 2 * NBLK], U8, name="wc%d" % n, align_bytes=64)
+            wc.append(wc_t)
+        xs = []
+        ws = []
+        for i, (lo, hi) in enumerate(X_PLANE_RANGES):
+            xs_t = keep.tile([P, PASSES, (hi - lo) * NBLK], U8, name="xs%d" % i, align_bytes=64)
+            xs.append(xs_t)
+        for i, (lo, hi) in enumerate(W_PLANE_RANGES):
+            ws_t = keep.tile([P, PASSES, (hi - lo) * NBLK], U8, name="ws%d" % i, align_bytes=64)
+            ws.append(ws_t)
+
+        eps_t = keep.tile([P, 1], F32, name="eps_t")
+        for plane in (xs[0], ws[0]):
+            nc.vector.memset(plane[:].rearrange("p g n -> p (g n)").bitcast(I32), 0)
+        nc.vector.memset(eps_t[:], EPS)
+        for plane in (ws[1], ws[2], xs[1]):
+            nc.vector.memset(plane[:].rearrange("p g n -> p (g n)").bitcast(I32), 0)
+
+        warm = keep.tile([P, 1], F32, name="warm")
+        nc.scalar.activation(out=warm[:], in_=eps_t[:], func=ACT.Abs_reciprocal_sqrt)
+
+        def load_codes(dst, src, c):
+            nc.sync.dma_start(
+                out=dst[:].bitcast(I32),
+                in_=src[:, :, c * 2 * NBLK : (c + 1) * 2 * NBLK].rearrange("g p n -> p g n").bitcast(I32),
+            )
+
+        def load_scales(dst, src, blocks, quads):
+            lo, hi = blocks
+            for quad in quads:
+                nc.sync.dma_start(
+                    out=dst[32 * quad : 32 * quad + 4, :, :].bitcast(I32),
+                    in_=src[:, 4 * quad : 4 * quad + 4, lo * NBLK : hi * NBLK]
+                    .rearrange("g r n -> r g n")
+                    .bitcast(I32),
+                )
+
+        load_scales(xs[0], x_scales, X_PLANE_RANGES[0], (0, 1))
+        load_codes(xc[0], x_words, 0)
+        load_codes(wc[0], wqkv_words, 0)
+        load_scales(xs[0], x_scales, X_PLANE_RANGES[0], (2, 3))
+        load_scales(ws[0], wqkv_scales, W_PLANE_RANGES[0], range(4))
+        load_codes(wc[1], wqkv_words, 1)
+        load_scales(ws[1], wqkv_scales, W_PLANE_RANGES[1], range(4))
+        load_codes(wc[2], wqkv_words, 2)
+        load_codes(wc[3], wqkv_words, 3)
+        load_scales(ws[2], wqkv_scales, W_PLANE_RANGES[2], range(4))
+        load_codes(wc[4], wqkv_words, 4)
+        load_codes(wc[5], wqkv_words, 5)
+        load_scales(xs[1], x_scales, X_PLANE_RANGES[1], range(4))
+        for c in range(1, GROUPS):
+            load_codes(xc[c], x_words, c)
+
+        def plane_cols(planes, ranges, blk, g, first_col, width):
+            for tile_i, (lo, hi) in enumerate(ranges):
+                if lo <= blk < hi:
+                    start = (blk - lo) * NBLK + first_col
+                    return planes[tile_i][:, g, start : start + width]
+            return None
+
+        swapped = {}
+        for key, w_b in (("q", wq_b), ("k", wk_b)):
+            wsw = keep.tile([P, HD // 2, 2], F32, name="wsw_" + key)
+            w_pairs = w_b[:].rearrange("p (j e) -> p j e", e=2)
+            nc.vector.tensor_scalar(
+                out=wsw[:, :, 0:1], in0=w_pairs[:, :, 1:2], scalar1=-1.0, scalar2=None, op0=ALU.mult
+            )
+            nc.vector.tensor_copy(out=wsw[:, :, 1:2], in_=w_pairs[:, :, 0:1])
+            swapped[key] = wsw
+
+        tabs = {}
+        full = [P, TPG, HD // 2, 2]
+
+        def build_tables(eng, m):
+            pairs = fc[:, TPG * m : TPG * (m + 1), :].rearrange("p t (j e) -> p t j e", e=2)
+            for key, w_b in (("q", wq_b), ("k", wk_b)):
+                ta = keep.tile([P, TPG, HD], F32, name="ta_%s%d" % (key, m))
+                tb = keep.tile([P, TPG, HD], F32, name="tb_%s%d" % (key, m))
+                eng.tensor_tensor(
+                    out=ta[:].rearrange("p t (j e) -> p t j e", e=2),
+                    in0=pairs[:, :, :, 0:1].to_broadcast(full),
+                    in1=w_b[:].rearrange("p (o j e) -> p o j e", o=1, e=2).to_broadcast(full),
+                    op=ALU.mult,
+                )
+                eng.tensor_tensor(
+                    out=tb[:].rearrange("p t (j e) -> p t j e", e=2),
+                    in0=pairs[:, :, :, 1:2].to_broadcast(full),
+                    in1=swapped[key][:].rearrange("p (o j) e -> p o j e", o=1).to_broadcast(full),
+                    op=ALU.mult,
+                )
+                tabs[(key, m)] = (ta, tb)
+
+        build_tables(nc.vector, 0)
+        build_tables(nc.gpsimd, 1)
+
+        out_q = out_0.rearrange("b s h d -> (b s) (h d)").rearrange("(c t p) n -> c p t n", t=TPG, p=P)
+        out_k = out_1.rearrange("b s h d -> (b s) (h d)").rearrange("(c t p) n -> c p t n", t=TPG, p=P)
+        out_v = out_2.rearrange("b s h d -> (b s) (h d)").rearrange("(i p) n -> i p n", p=P)
+
+        def project(c, t, n):
+            acc = psum.tile([P, NBLK], F32, name="acc")
+            for g in range(PASSES):
+                nc.tensor.matmul_mx(
+                    out=acc[:],
+                    lhsT=xc[c][:, g, t * 2 * P : (t + 1) * 2 * P].bitcast(FP4X4),
+                    lhsT_scale=plane_cols(xs, X_PLANE_RANGES, c, g, t * P, P),
+                    rhs=wc[n][:, g, :].bitcast(FP4X4),
+                    rhs_scale=plane_cols(ws, W_PLANE_RANGES, n, g, 0, NBLK),
+                    start=(g == 0),
+                    stop=(g == PASSES - 1),
+                )
+            return acc
+
+        def v_bank(i):
+            acc = project(i // TPG, i % TPG, V_BLOCK)
+            vt = work.tile([P, NBLK], F32, name="vt")
+            nc.scalar.copy(out=vt[:], in_=acc[:])
+            nc.scalar.dma_start(out=out_v[i], in_=vt[:])
+
+        def qk_block(c, n):
+            pt = work.tile([P, TPG, NBLK], F32, name="pt")
+            qt = work.tile([P, TPG, NBLK], F32, name="qt")
+            ta, tb = tabs[("k" if n == K_BLOCK else "q", c % POS_GROUPS)]
+            for t in range(TPG):
+                acc = project(c, t, n)
+                ms = small.tile([P, HEADS_PER_BLK], F32, name="ms")
+                rstd = small.tile([P, HEADS_PER_BLK], F32, name="rstd")
+                for h in range(HEADS_PER_BLK):
+                    junk = small.tile([P, HD], BF16, name="junk", bufs=2)
+                    nc.scalar.activation(
+                        out=junk[:],
+                        in_=acc[:, h * HD : (h + 1) * HD],
+                        func=ACT.Square,
+                        scale=INV_SQRT_HD,
+                        accum_out=ms[:, h : h + 1],
+                    )
+                nc.scalar.activation(out=rstd[:], in_=ms[:], func=ACT.Abs_reciprocal_sqrt, bias=eps_t[:])
+                for h in range(HEADS_PER_BLK):
+                    cols = slice(h * HD, (h + 1) * HD)
+                    nc.vector.scalar_tensor_tensor(
+                        out=pt[:, t, cols],
+                        in0=acc[:, cols],
+                        scalar=rstd[:, h : h + 1],
+                        in1=ta[:, t, :],
+                        op0=ALU.mult,
+                        op1=ALU.mult,
+                    )
+                    nc.vector.scalar_tensor_tensor(
+                        out=qt[:, t, cols].rearrange("p (j e) -> p j e", e=2),
+                        in0=acc[:, cols].rearrange("p (j e) -> p j e", e=2)[:, :, ::-1],
+                        scalar=rstd[:, h : h + 1],
+                        in1=tb[:, t, :].rearrange("p (j e) -> p j e", e=2),
+                        op0=ALU.mult,
+                        op1=ALU.mult,
+                    )
+            nc.gpsimd.tensor_tensor(
+                out=pt[:].rearrange("p t n -> p (t n)"),
+                in0=pt[:].rearrange("p t n -> p (t n)"),
+                in1=qt[:].rearrange("p t n -> p (t n)"),
+                op=ALU.add,
+            )
+            if n == K_BLOCK:
+                nc.sync.dma_start(out=out_k[c], in_=pt[:])
+            else:
+                nc.sync.dma_start(out=out_q[c][:, :, n * NBLK : (n + 1) * NBLK], in_=pt[:])
+
+        v_done = 0
+        for c in range(GROUPS):
+            for n in range(V_BLOCK):
+                qk_block(c, n)
+                if (c * V_BLOCK + n) % 2 == 1:
+                    v_bank(v_done)
+                    v_done += 1
+                if c == 0 and n == 1:
+                    build_tables(nc.gpsimd, 2)
+        for i in range(v_done, TOKEN_TILES):
+            v_bank(i)

@@ -28,6 +28,8 @@ EPS = 1e-6
 INV_SQRT_HD = 1.0 / (128.0 ** 0.5)
 W_PLANE_RANGES = ((0, 1), (1, 3), (3, 6))
 X_PLANE_RANGES = ((0, 1), (1, 6))
+WARM_BEFORE = 10
+WARM_AFTER = 2
 
 FLOPS = 2 * TOKENS * D_IN * 3072
 
@@ -42,13 +44,15 @@ def tile_attention_pa_kernel(
         small = ctx.enter_context(tc.tile_pool(name="small", bufs=8))
         psum = ctx.enter_context(tc.psum_pool(name="psum", bufs=8))
 
-        wq_b = keep.tile([P, HD], BF16, name="wq_b")
-        wk_b = keep.tile([P, HD], BF16, name="wk_b")
+        ones = keep.tile([P, P], BF16, name="ones")
+        idle_rhs = keep.tile([P, NBLK], BF16, name="idle_rhs")
+        w_rows = keep.tile([P, 2 * HD], BF16, name="w_rows")
+        nc.gpsimd.memset(w_rows[:], 0.0)
+        nc.gpsimd.dma_start(out=w_rows[0:1, 0:HD], in_=q_norm_w.rearrange("(o d) -> o d", o=1))
+        nc.gpsimd.dma_start(out=w_rows[0:1, HD : 2 * HD], in_=k_norm_w.rearrange("(o d) -> o d", o=1))
         fc = keep.tile([P, 12, HD], BF16, name="fc")
         fc_view = freqs_cis.rearrange("(t p) j e -> p t (j e)", p=P)
-        nc.gpsimd.dma_start(out=wq_b[:], in_=q_norm_w.partition_broadcast(P))
         nc.gpsimd.dma_start(out=fc[:, 0:4, :], in_=fc_view[:, 0:4, :])
-        nc.gpsimd.dma_start(out=wk_b[:], in_=k_norm_w.partition_broadcast(P))
         nc.gpsimd.dma_start(out=fc[:, 4:12, :], in_=fc_view[:, 4:12, :])
 
         xc = []
@@ -71,6 +75,8 @@ def tile_attention_pa_kernel(
         eps_t = keep.tile([P, 1], F32, name="eps_t")
         for plane in (xs[0], ws[0]):
             nc.vector.memset(plane[:].rearrange("p g n -> p (g n)").bitcast(I32), 0)
+        nc.vector.memset(ones[:], 1.0)
+        nc.vector.memset(idle_rhs[:], 0.0)
         nc.vector.memset(eps_t[:], EPS)
         for plane in (ws[1], ws[2], xs[1]):
             nc.vector.memset(plane[:].rearrange("p g n -> p (g n)").bitcast(I32), 0)
@@ -117,34 +123,42 @@ def tile_attention_pa_kernel(
                     return planes[tile_i][:, g, start : start + width]
             return None
 
-        swapped = {}
-        for key, w_b in (("q", wq_b), ("k", wk_b)):
-            wsw = keep.tile([P, HD // 2, 2], F32, name="wsw_" + key)
-            w_pairs = w_b[:].rearrange("p (j e) -> p j e", e=2)
-            nc.vector.tensor_scalar(
-                out=wsw[:, :, 0:1], in0=w_pairs[:, :, 1:2], scalar1=-1.0, scalar2=None, op0=ALU.mult
-            )
-            nc.vector.tensor_copy(out=wsw[:, :, 1:2], in_=w_pairs[:, :, 0:1])
-            swapped[key] = wsw
+        idle_ps = psum.tile([P, NBLK], F32, name="acc")
+        for i in range(WARM_BEFORE):
+            nc.tensor.matmul(out=idle_ps[:], lhsT=ones[:], rhs=idle_rhs[:], start=True, stop=True)
+        w_ps = psum.tile([P, NBLK], F32, name="acc")
+        nc.tensor.matmul(out=w_ps[:, 0 : 2 * HD], lhsT=ones[:], rhs=w_rows[:], start=True, stop=True)
+        idle_ps2 = psum.tile([P, NBLK], F32, name="acc")
+        for i in range(WARM_AFTER):
+            nc.tensor.matmul(out=idle_ps2[:], lhsT=ones[:], rhs=idle_rhs[:], start=True, stop=True)
+
+        w_all = keep.tile([P, 2, HD // 2, 2], F32, name="w_all")
+        w_swp = keep.tile([P, 2, HD // 2, 2], F32, name="w_swp")
+        w_ps_v = w_ps[:, 0 : 2 * HD].rearrange("p (k j e) -> p k j e", k=2, e=2)
+        nc.vector.tensor_copy(out=w_all[:], in_=w_ps_v)
+        nc.vector.tensor_scalar(
+            out=w_swp[:, :, :, 0:1], in0=w_ps_v[:, :, :, 1:2], scalar1=-1.0, scalar2=None, op0=ALU.mult
+        )
+        nc.vector.tensor_copy(out=w_swp[:, :, :, 1:2], in_=w_ps_v[:, :, :, 0:1])
 
         tabs = {}
         full = [P, TPG, HD // 2, 2]
 
         def build_tables(eng, m):
             pairs = fc[:, TPG * m : TPG * (m + 1), :].rearrange("p t (j e) -> p t j e", e=2)
-            for key, w_b in (("q", wq_b), ("k", wk_b)):
+            for ki, key in enumerate(("q", "k")):
                 ta = keep.tile([P, TPG, HD], F32, name="ta_%s%d" % (key, m))
                 tb = keep.tile([P, TPG, HD], F32, name="tb_%s%d" % (key, m))
                 eng.tensor_tensor(
                     out=ta[:].rearrange("p t (j e) -> p t j e", e=2),
                     in0=pairs[:, :, :, 0:1].to_broadcast(full),
-                    in1=w_b[:].rearrange("p (o j e) -> p o j e", o=1, e=2).to_broadcast(full),
+                    in1=w_all[:, ki : ki + 1, :, :].to_broadcast(full),
                     op=ALU.mult,
                 )
                 eng.tensor_tensor(
                     out=tb[:].rearrange("p t (j e) -> p t j e", e=2),
                     in0=pairs[:, :, :, 1:2].to_broadcast(full),
-                    in1=swapped[key][:].rearrange("p (o j) e -> p o j e", o=1).to_broadcast(full),
+                    in1=w_swp[:, ki : ki + 1, :, :].to_broadcast(full),
                     op=ALU.mult,
                 )
                 tabs[(key, m)] = (ta, tb)
@@ -172,18 +186,24 @@ def tile_attention_pa_kernel(
 
         def v_bank(i):
             acc = project(i // TPG, i % TPG, V_BLOCK)
-            vt = work.tile([P, NBLK], F32, name="vt")
+            vt = work.tile([P, NBLK], F32, name="vt", bufs=10)
             nc.scalar.copy(out=vt[:], in_=acc[:])
-            nc.scalar.dma_start(out=out_v[i], in_=vt[:])
+            nc.sync.dma_start(out=out_v[i], in_=vt[:])
 
-        def qk_block(c, n):
-            pt = work.tile([P, TPG, NBLK], F32, name="pt")
+        def out_block(c, n):
+            if n == K_BLOCK:
+                return out_k[c]
+            return out_q[c][:, :, n * NBLK : (n + 1) * NBLK]
+
+        def qk_block(c, n, wide, last):
+            pt = work.tile([P, TPG, NBLK], F32, name="pt", bufs=6)
             qt = work.tile([P, TPG, NBLK], F32, name="qt")
             ta, tb = tabs[("k" if n == K_BLOCK else "q", c % POS_GROUPS)]
+            rstd = small.tile([P, TPG, HEADS_PER_BLK], F32, name="rstd")
+            by_head = [P, HEADS_PER_BLK, HD // 2, 2]
             for t in range(TPG):
                 acc = project(c, t, n)
                 ms = small.tile([P, HEADS_PER_BLK], F32, name="ms")
-                rstd = small.tile([P, HEADS_PER_BLK], F32, name="rstd")
                 for h in range(HEADS_PER_BLK):
                     junk = small.tile([P, HD], BF16, name="junk", bufs=2)
                     nc.scalar.activation(
@@ -193,13 +213,30 @@ def tile_attention_pa_kernel(
                         scale=INV_SQRT_HD,
                         accum_out=ms[:, h : h + 1],
                     )
-                nc.scalar.activation(out=rstd[:], in_=ms[:], func=ACT.Abs_reciprocal_sqrt, bias=eps_t[:])
+                nc.scalar.activation(
+                    out=rstd[:, t, :], in_=ms[:], func=ACT.Abs_reciprocal_sqrt, bias=eps_t[:]
+                )
+                if wide:
+                    acc4 = acc[:].rearrange("p (h j e) -> p h j e", h=HEADS_PER_BLK, e=2)
+                    nc.vector.tensor_tensor(
+                        out=pt[:, t, :].rearrange("p (h j e) -> p h j e", h=HEADS_PER_BLK, e=2),
+                        in0=acc4,
+                        in1=ta[:, t : t + 1, :].rearrange("p o (j e) -> p o j e", e=2).to_broadcast(by_head),
+                        op=ALU.mult,
+                    )
+                    nc.vector.tensor_tensor(
+                        out=qt[:, t, :].rearrange("p (h j e) -> p h j e", h=HEADS_PER_BLK, e=2),
+                        in0=acc4[:, :, :, ::-1],
+                        in1=tb[:, t : t + 1, :].rearrange("p o (j e) -> p o j e", e=2).to_broadcast(by_head),
+                        op=ALU.mult,
+                    )
+                    continue
                 for h in range(HEADS_PER_BLK):
                     cols = slice(h * HD, (h + 1) * HD)
                     nc.vector.scalar_tensor_tensor(
                         out=pt[:, t, cols],
                         in0=acc[:, cols],
-                        scalar=rstd[:, h : h + 1],
+                        scalar=rstd[:, t, h : h + 1],
                         in1=ta[:, t, :],
                         op0=ALU.mult,
                         op1=ALU.mult,
@@ -207,30 +244,59 @@ def tile_attention_pa_kernel(
                     nc.vector.scalar_tensor_tensor(
                         out=qt[:, t, cols].rearrange("p (j e) -> p j e", e=2),
                         in0=acc[:, cols].rearrange("p (j e) -> p j e", e=2)[:, :, ::-1],
-                        scalar=rstd[:, h : h + 1],
+                        scalar=rstd[:, t, h : h + 1],
                         in1=tb[:, t, :].rearrange("p (j e) -> p j e", e=2),
                         op0=ALU.mult,
                         op1=ALU.mult,
                     )
+            if last:
+                for t in range(0, TPG, 2):
+                    nc.vector.tensor_tensor(
+                        out=pt[:, t : t + 2, :], in0=pt[:, t : t + 2, :], in1=qt[:, t : t + 2, :], op=ALU.add
+                    )
+                    nc.sync.dma_start(out=out_block(c, n)[:, t : t + 2, :], in_=pt[:, t : t + 2, :])
+                return None
             nc.gpsimd.tensor_tensor(
                 out=pt[:].rearrange("p t n -> p (t n)"),
                 in0=pt[:].rearrange("p t n -> p (t n)"),
                 in1=qt[:].rearrange("p t n -> p (t n)"),
                 op=ALU.add,
             )
-            if n == K_BLOCK:
-                nc.sync.dma_start(out=out_k[c], in_=pt[:])
-            else:
-                nc.sync.dma_start(out=out_q[c][:, :, n * NBLK : (n + 1) * NBLK], in_=pt[:])
+            if wide:
+                return (pt, rstd, c, n)
+            nc.sync.dma_start(out=out_block(c, n), in_=pt[:])
+            return None
+
+        def finish_wide(todo):
+            pt, rstd, c, n = todo
+            for t in range(TPG):
+                for h in range(HEADS_PER_BLK):
+                    cols = slice(h * HD, (h + 1) * HD)
+                    nc.scalar.activation(
+                        out=pt[:, t, cols], in_=pt[:, t, cols], func=ACT.Copy, scale=rstd[:, t, h : h + 1]
+                    )
+            nc.sync.dma_start(out=out_block(c, n), in_=pt[:])
 
         v_done = 0
-        for c in range(GROUPS):
-            for n in range(V_BLOCK):
-                qk_block(c, n)
-                if (c * V_BLOCK + n) % 2 == 1:
-                    v_bank(v_done)
-                    v_done += 1
-                if c == 0 and n == 1:
-                    build_tables(nc.gpsimd, 2)
+        waiting = []
+        finished = 0
+        n_blocks = GROUPS * V_BLOCK
+        for b in range(n_blocks):
+            c = b // V_BLOCK
+            n = b % V_BLOCK
+            todo = qk_block(c, n, False, b == n_blocks - 1)
+            if todo is not None:
+                waiting.append(todo)
+            if finished < len(waiting) and waiting[finished][2] * V_BLOCK + waiting[finished][3] <= b - 2:
+                finish_wide(waiting[finished])
+                finished += 1
+            if b % 2 == 1:
+                v_bank(v_done)
+                v_done += 1
+            if b == 1:
+                build_tables(nc.gpsimd, 2)
         for i in range(v_done, TOKEN_TILES):
             v_bank(i)
+            if finished < len(waiting):
+                finish_wide(waiting[finished])
+                finished += 1

@@ -30,8 +30,15 @@ W_PLANE_RANGES = ((0, 1), (1, 3), (3, 6))
 X_PLANE_RANGES = ((0, 1), (1, 6))
 WARM_BEFORE = 10
 WARM_AFTER = 2
+QK_BLOCKS = GROUPS * V_BLOCK
+SCALE_LAG = 3
+SCALES_PER_BANK = 2
 
 FLOPS = 2 * TOKENS * D_IN * 3072
+
+
+def is_wide(b):
+    return b % 2 == 0 and b <= 24
 
 
 def tile_attention_pa_kernel(
@@ -40,8 +47,11 @@ def tile_attention_pa_kernel(
     nc = tc.nc
     with ExitStack() as ctx:
         keep = ctx.enter_context(tc.tile_pool(name="keep", bufs=1))
-        work = ctx.enter_context(tc.tile_pool(name="work", bufs=4))
-        small = ctx.enter_context(tc.tile_pool(name="small", bufs=8))
+        pt_pool = ctx.enter_context(tc.tile_pool(name="pt_pool", bufs=7))
+        qt_pool = ctx.enter_context(tc.tile_pool(name="qt_pool", bufs=4))
+        vt_pool = ctx.enter_context(tc.tile_pool(name="vt_pool", bufs=10))
+        stats = ctx.enter_context(tc.tile_pool(name="stats", bufs=8))
+        junk_pool = ctx.enter_context(tc.tile_pool(name="junk_pool", bufs=2))
         psum = ctx.enter_context(tc.psum_pool(name="psum", bufs=8))
 
         ones = keep.tile([P, P], BF16, name="ones")
@@ -144,31 +154,49 @@ def tile_attention_pa_kernel(
         tabs = {}
         full = [P, TPG, HD // 2, 2]
 
-        def build_tables(eng, m):
+        def table_step(eng, m, ki, part):
             pairs = fc[:, TPG * m : TPG * (m + 1), :].rearrange("p t (j e) -> p t j e", e=2)
-            for ki, key in enumerate(("q", "k")):
-                ta = keep.tile([P, TPG, HD], F32, name="ta_%s%d" % (key, m))
-                tb = keep.tile([P, TPG, HD], F32, name="tb_%s%d" % (key, m))
-                eng.tensor_tensor(
-                    out=ta[:].rearrange("p t (j e) -> p t j e", e=2),
-                    in0=pairs[:, :, :, 0:1].to_broadcast(full),
-                    in1=w_all[:, ki : ki + 1, :, :].to_broadcast(full),
-                    op=ALU.mult,
-                )
-                eng.tensor_tensor(
-                    out=tb[:].rearrange("p t (j e) -> p t j e", e=2),
-                    in0=pairs[:, :, :, 1:2].to_broadcast(full),
-                    in1=w_swp[:, ki : ki + 1, :, :].to_broadcast(full),
-                    op=ALU.mult,
-                )
-                tabs[(key, m)] = (ta, tb)
+            tab = keep.tile([P, TPG, HD], F32, name="tab_%d_%d_%d" % (m, ki, part))
+            gains = w_all if part == 0 else w_swp
+            eng.tensor_tensor(
+                out=tab[:].rearrange("p t (j e) -> p t j e", e=2),
+                in0=pairs[:, :, :, part : part + 1].to_broadcast(full),
+                in1=gains[:, ki : ki + 1, :, :].to_broadcast(full),
+                op=ALU.mult,
+            )
+            tabs[(m, ki, part)] = tab
 
-        build_tables(nc.vector, 0)
-        build_tables(nc.gpsimd, 1)
+        for m, eng in ((0, nc.vector), (1, nc.gpsimd)):
+            for ki in range(2):
+                for part in range(2):
+                    table_step(eng, m, ki, part)
 
         out_q = out_0.rearrange("b s h d -> (b s) (h d)").rearrange("(c t p) n -> c p t n", t=TPG, p=P)
         out_k = out_1.rearrange("b s h d -> (b s) (h d)").rearrange("(c t p) n -> c p t n", t=TPG, p=P)
         out_v = out_2.rearrange("b s h d -> (b s) (h d)").rearrange("(i p) n -> i p n", p=P)
+
+        def out_block(b):
+            c = b // V_BLOCK
+            n = b % V_BLOCK
+            if n == K_BLOCK:
+                return out_k[c]
+            return out_q[c][:, :, n * NBLK : (n + 1) * NBLK]
+
+        jobs = []
+        cursor = [0]
+
+        def late_scalings(b, count):
+            for i in range(count):
+                if cursor[0] >= len(jobs) or jobs[cursor[0]][0] > b - SCALE_LAG:
+                    return
+                src_b, pt, rstd, t, h = jobs[cursor[0]]
+                cursor[0] += 1
+                cols = slice(h * HD, (h + 1) * HD)
+                nc.scalar.activation(
+                    out=pt[:, t, cols], in_=pt[:, t, cols], func=ACT.Copy, scale=rstd[:, t, h : h + 1]
+                )
+                if h == HEADS_PER_BLK - 1 and t % 2 == 1:
+                    nc.sync.dma_start(out=out_block(src_b)[:, t - 1 : t + 1, :], in_=pt[:, t - 1 : t + 1, :])
 
         def project(c, t, n):
             acc = psum.tile([P, NBLK], F32, name="acc")
@@ -184,39 +212,38 @@ def tile_attention_pa_kernel(
                 )
             return acc
 
-        def v_bank(i):
+        def v_bank(i, b):
             acc = project(i // TPG, i % TPG, V_BLOCK)
-            vt = work.tile([P, NBLK], F32, name="vt", bufs=10)
+            vt = vt_pool.tile([P, NBLK], F32, name="vt")
             nc.scalar.copy(out=vt[:], in_=acc[:])
             nc.sync.dma_start(out=out_v[i], in_=vt[:])
+            late_scalings(b, SCALES_PER_BANK)
 
-        def out_block(c, n):
-            if n == K_BLOCK:
-                return out_k[c]
-            return out_q[c][:, :, n * NBLK : (n + 1) * NBLK]
-
-        def qk_block(c, n, wide, last):
-            pt = work.tile([P, TPG, NBLK], F32, name="pt", bufs=6)
-            qt = work.tile([P, TPG, NBLK], F32, name="qt")
-            ta, tb = tabs[("k" if n == K_BLOCK else "q", c % POS_GROUPS)]
-            rstd = small.tile([P, TPG, HEADS_PER_BLK], F32, name="rstd")
+        def qk_block(b):
+            c = b // V_BLOCK
+            n = b % V_BLOCK
+            wide = is_wide(b)
+            pt = pt_pool.tile([P, TPG, NBLK], F32, name="pt")
+            qt = qt_pool.tile([P, TPG, NBLK], F32, name="qt")
+            ki = 1 if n == K_BLOCK else 0
+            ta = tabs[(c % POS_GROUPS, ki, 0)]
+            tb = tabs[(c % POS_GROUPS, ki, 1)]
+            ms = stats.tile([P, TPG, HEADS_PER_BLK], F32, name="ms")
+            rstd = stats.tile([P, TPG, HEADS_PER_BLK], F32, name="rstd")
             by_head = [P, HEADS_PER_BLK, HD // 2, 2]
             for t in range(TPG):
                 acc = project(c, t, n)
-                ms = small.tile([P, HEADS_PER_BLK], F32, name="ms")
                 for h in range(HEADS_PER_BLK):
-                    junk = small.tile([P, HD], BF16, name="junk", bufs=2)
+                    junk = junk_pool.tile([P, HD], BF16, name="junk")
                     nc.scalar.activation(
                         out=junk[:],
                         in_=acc[:, h * HD : (h + 1) * HD],
                         func=ACT.Square,
                         scale=INV_SQRT_HD,
-                        accum_out=ms[:, h : h + 1],
+                        accum_out=ms[:, t, h : h + 1],
                     )
-                nc.scalar.activation(
-                    out=rstd[:, t, :], in_=ms[:], func=ACT.Abs_reciprocal_sqrt, bias=eps_t[:]
-                )
                 if wide:
+                    late_scalings(b, SCALES_PER_BANK)
                     acc4 = acc[:].rearrange("p (h j e) -> p h j e", h=HEADS_PER_BLK, e=2)
                     nc.vector.tensor_tensor(
                         out=pt[:, t, :].rearrange("p (h j e) -> p h j e", h=HEADS_PER_BLK, e=2),
@@ -231,6 +258,10 @@ def tile_attention_pa_kernel(
                         op=ALU.mult,
                     )
                     continue
+                nc.scalar.activation(
+                    out=rstd[:, t, :], in_=ms[:, t, :], func=ACT.Abs_reciprocal_sqrt, bias=eps_t[:]
+                )
+                late_scalings(b, SCALES_PER_BANK)
                 for h in range(HEADS_PER_BLK):
                     cols = slice(h * HD, (h + 1) * HD)
                     nc.vector.scalar_tensor_tensor(
@@ -249,13 +280,13 @@ def tile_attention_pa_kernel(
                         op0=ALU.mult,
                         op1=ALU.mult,
                     )
-            if last:
+            if b == QK_BLOCKS - 1:
                 for t in range(0, TPG, 2):
                     nc.vector.tensor_tensor(
                         out=pt[:, t : t + 2, :], in0=pt[:, t : t + 2, :], in1=qt[:, t : t + 2, :], op=ALU.add
                     )
-                    nc.sync.dma_start(out=out_block(c, n)[:, t : t + 2, :], in_=pt[:, t : t + 2, :])
-                return None
+                    nc.sync.dma_start(out=out_block(b)[:, t : t + 2, :], in_=pt[:, t : t + 2, :])
+                return
             nc.gpsimd.tensor_tensor(
                 out=pt[:].rearrange("p t n -> p (t n)"),
                 in0=pt[:].rearrange("p t n -> p (t n)"),
@@ -263,40 +294,26 @@ def tile_attention_pa_kernel(
                 op=ALU.add,
             )
             if wide:
-                return (pt, rstd, c, n)
-            nc.sync.dma_start(out=out_block(c, n), in_=pt[:])
-            return None
-
-        def finish_wide(todo):
-            pt, rstd, c, n = todo
-            for t in range(TPG):
-                for h in range(HEADS_PER_BLK):
-                    cols = slice(h * HD, (h + 1) * HD)
-                    nc.scalar.activation(
-                        out=pt[:, t, cols], in_=pt[:, t, cols], func=ACT.Copy, scale=rstd[:, t, h : h + 1]
-                    )
-            nc.sync.dma_start(out=out_block(c, n), in_=pt[:])
+                nc.scalar.activation(
+                    out=rstd[:].rearrange("p t h -> p (t h)"),
+                    in_=ms[:].rearrange("p t h -> p (t h)"),
+                    func=ACT.Abs_reciprocal_sqrt,
+                    bias=eps_t[:],
+                )
+                for t in range(TPG):
+                    for h in range(HEADS_PER_BLK):
+                        jobs.append((b, pt, rstd, t, h))
+                return
+            nc.sync.dma_start(out=out_block(b), in_=pt[:])
 
         v_done = 0
-        waiting = []
-        finished = 0
-        n_blocks = GROUPS * V_BLOCK
-        for b in range(n_blocks):
-            c = b // V_BLOCK
-            n = b % V_BLOCK
-            todo = qk_block(c, n, False, b == n_blocks - 1)
-            if todo is not None:
-                waiting.append(todo)
-            if finished < len(waiting) and waiting[finished][2] * V_BLOCK + waiting[finished][3] <= b - 2:
-                finish_wide(waiting[finished])
-                finished += 1
-            if b % 2 == 1:
-                v_bank(v_done)
-                v_done += 1
-            if b == 1:
-                build_tables(nc.gpsimd, 2)
-        for i in range(v_done, TOKEN_TILES):
-            v_bank(i)
-            if finished < len(waiting):
-                finish_wide(waiting[finished])
-                finished += 1
+        with tc.manual_schedule():
+            for b in range(QK_BLOCKS):
+                qk_block(b)
+                if b % 2 == 1:
+                    v_bank(v_done, b)
+                    v_done += 1
+                if b % 2 == 1 and b < 8:
+                    table_step(nc.gpsimd, 2, (b // 2) // 2, (b // 2) % 2)
+            for i in range(v_done, TOKEN_TILES):
+                v_bank(i, QK_BLOCKS + SCALE_LAG)

@@ -31,14 +31,9 @@ X_PLANE_RANGES = ((0, 1), (1, 6))
 WARM_BEFORE = 10
 WARM_AFTER = 2
 QK_BLOCKS = GROUPS * V_BLOCK
-SCALE_LAG = 3
-SCALES_PER_BANK = 2
+V_AFTER = (1, 3, 4)
 
 FLOPS = 2 * TOKENS * D_IN * 3072
-
-
-def is_wide(b):
-    return b % 2 == 0 and b <= 24
 
 
 def tile_attention_pa_kernel(
@@ -47,11 +42,11 @@ def tile_attention_pa_kernel(
     nc = tc.nc
     with ExitStack() as ctx:
         keep = ctx.enter_context(tc.tile_pool(name="keep", bufs=1))
-        pt_pool = ctx.enter_context(tc.tile_pool(name="pt_pool", bufs=7))
+        pt_pool = ctx.enter_context(tc.tile_pool(name="pt_pool", bufs=6))
         qt_pool = ctx.enter_context(tc.tile_pool(name="qt_pool", bufs=4))
         vt_pool = ctx.enter_context(tc.tile_pool(name="vt_pool", bufs=10))
-        stats = ctx.enter_context(tc.tile_pool(name="stats", bufs=8))
-        junk_pool = ctx.enter_context(tc.tile_pool(name="junk_pool", bufs=2))
+        stats = ctx.enter_context(tc.tile_pool(name="stats", bufs=4))
+        junk_pool = ctx.enter_context(tc.tile_pool(name="junk_pool", bufs=8))
         psum = ctx.enter_context(tc.psum_pool(name="psum", bufs=8))
 
         ones = keep.tile([P, P], BF16, name="ones")
@@ -118,10 +113,10 @@ def tile_attention_pa_kernel(
         load_codes(wc[1], wqkv_words, 1)
         load_scales(ws[1], wqkv_scales, W_PLANE_RANGES[1], range(4))
         load_codes(wc[2], wqkv_words, 2)
-        load_codes(wc[3], wqkv_words, 3)
         load_scales(ws[2], wqkv_scales, W_PLANE_RANGES[2], range(4))
-        load_codes(wc[4], wqkv_words, 4)
         load_codes(wc[5], wqkv_words, 5)
+        load_codes(wc[3], wqkv_words, 3)
+        load_codes(wc[4], wqkv_words, 4)
         load_scales(xs[1], x_scales, X_PLANE_RANGES[1], range(4))
         for c in range(1, GROUPS):
             load_codes(xc[c], x_words, c)
@@ -182,22 +177,6 @@ def tile_attention_pa_kernel(
                 return out_k[c]
             return out_q[c][:, :, n * NBLK : (n + 1) * NBLK]
 
-        jobs = []
-        cursor = [0]
-
-        def late_scalings(b, count):
-            for i in range(count):
-                if cursor[0] >= len(jobs) or jobs[cursor[0]][0] > b - SCALE_LAG:
-                    return
-                src_b, pt, rstd, t, h = jobs[cursor[0]]
-                cursor[0] += 1
-                cols = slice(h * HD, (h + 1) * HD)
-                nc.scalar.activation(
-                    out=pt[:, t, cols], in_=pt[:, t, cols], func=ACT.Copy, scale=rstd[:, t, h : h + 1]
-                )
-                if h == HEADS_PER_BLK - 1 and t % 2 == 1:
-                    nc.sync.dma_start(out=out_block(src_b)[:, t - 1 : t + 1, :], in_=pt[:, t - 1 : t + 1, :])
-
         def project(c, t, n):
             acc = psum.tile([P, NBLK], F32, name="acc")
             for g in range(PASSES):
@@ -212,27 +191,73 @@ def tile_attention_pa_kernel(
                 )
             return acc
 
-        def v_bank(i, b):
+        waiting = []
+
+        def second_half():
+            if len(waiting) == 0:
+                return
+            b, t, acc, ms, rstd, pt, qt = waiting[0]
+            waiting.clear()
+            ki = 1 if b % V_BLOCK == K_BLOCK else 0
+            ta = tabs[((b // V_BLOCK) % POS_GROUPS, ki, 0)]
+            tb = tabs[((b // V_BLOCK) % POS_GROUPS, ki, 1)]
+            nc.scalar.activation(
+                out=rstd[:, t, :], in_=ms[:, t, :], func=ACT.Abs_reciprocal_sqrt, bias=eps_t[:]
+            )
+            for h in range(HEADS_PER_BLK):
+                cols = slice(h * HD, (h + 1) * HD)
+                nc.vector.scalar_tensor_tensor(
+                    out=pt[:, t, cols],
+                    in0=acc[:, cols],
+                    scalar=rstd[:, t, h : h + 1],
+                    in1=ta[:, t, :],
+                    op0=ALU.mult,
+                    op1=ALU.mult,
+                )
+                nc.vector.scalar_tensor_tensor(
+                    out=qt[:, t, cols].rearrange("p (j e) -> p j e", e=2),
+                    in0=acc[:, cols].rearrange("p (j e) -> p j e", e=2)[:, :, ::-1],
+                    scalar=rstd[:, t, h : h + 1],
+                    in1=tb[:, t, :].rearrange("p (j e) -> p j e", e=2),
+                    op0=ALU.mult,
+                    op1=ALU.mult,
+                )
+            if t < TPG - 1:
+                return
+            if b == QK_BLOCKS - 1:
+                for half in range(0, TPG, 2):
+                    nc.vector.tensor_tensor(
+                        out=pt[:, half : half + 2, :],
+                        in0=pt[:, half : half + 2, :],
+                        in1=qt[:, half : half + 2, :],
+                        op=ALU.add,
+                    )
+                    nc.sync.dma_start(out=out_block(b)[:, half : half + 2, :], in_=pt[:, half : half + 2, :])
+                return
+            nc.gpsimd.tensor_tensor(
+                out=pt[:].rearrange("p t n -> p (t n)"),
+                in0=pt[:].rearrange("p t n -> p (t n)"),
+                in1=qt[:].rearrange("p t n -> p (t n)"),
+                op=ALU.add,
+            )
+            nc.sync.dma_start(out=out_block(b), in_=pt[:])
+            if b % 2 == 1 and b < 8:
+                table_step(nc.gpsimd, 2, (b // 2) // 2, (b // 2) % 2)
+
+        def v_bank(i):
             acc = project(i // TPG, i % TPG, V_BLOCK)
             vt = vt_pool.tile([P, NBLK], F32, name="vt")
             nc.scalar.copy(out=vt[:], in_=acc[:])
             nc.sync.dma_start(out=out_v[i], in_=vt[:])
-            late_scalings(b, SCALES_PER_BANK)
+            second_half()
 
         def qk_block(b):
-            c = b // V_BLOCK
-            n = b % V_BLOCK
-            wide = is_wide(b)
             pt = pt_pool.tile([P, TPG, NBLK], F32, name="pt")
             qt = qt_pool.tile([P, TPG, NBLK], F32, name="qt")
-            ki = 1 if n == K_BLOCK else 0
-            ta = tabs[(c % POS_GROUPS, ki, 0)]
-            tb = tabs[(c % POS_GROUPS, ki, 1)]
             ms = stats.tile([P, TPG, HEADS_PER_BLK], F32, name="ms")
             rstd = stats.tile([P, TPG, HEADS_PER_BLK], F32, name="rstd")
-            by_head = [P, HEADS_PER_BLK, HD // 2, 2]
             for t in range(TPG):
-                acc = project(c, t, n)
+                acc = project(b // V_BLOCK, t, b % V_BLOCK)
                 for h in range(HEADS_PER_BLK):
                     junk = junk_pool.tile([P, HD], BF16, name="junk")
                     nc.scalar.activation(
@@ -242,78 +267,15 @@ def tile_attention_pa_kernel(
                         scale=INV_SQRT_HD,
                         accum_out=ms[:, t, h : h + 1],
                     )
-                if wide:
-                    late_scalings(b, SCALES_PER_BANK)
-                    acc4 = acc[:].rearrange("p (h j e) -> p h j e", h=HEADS_PER_BLK, e=2)
-                    nc.vector.tensor_tensor(
-                        out=pt[:, t, :].rearrange("p (h j e) -> p h j e", h=HEADS_PER_BLK, e=2),
-                        in0=acc4,
-                        in1=ta[:, t : t + 1, :].rearrange("p o (j e) -> p o j e", e=2).to_broadcast(by_head),
-                        op=ALU.mult,
-                    )
-                    nc.vector.tensor_tensor(
-                        out=qt[:, t, :].rearrange("p (h j e) -> p h j e", h=HEADS_PER_BLK, e=2),
-                        in0=acc4[:, :, :, ::-1],
-                        in1=tb[:, t : t + 1, :].rearrange("p o (j e) -> p o j e", e=2).to_broadcast(by_head),
-                        op=ALU.mult,
-                    )
-                    continue
-                nc.scalar.activation(
-                    out=rstd[:, t, :], in_=ms[:, t, :], func=ACT.Abs_reciprocal_sqrt, bias=eps_t[:]
-                )
-                late_scalings(b, SCALES_PER_BANK)
-                for h in range(HEADS_PER_BLK):
-                    cols = slice(h * HD, (h + 1) * HD)
-                    nc.vector.scalar_tensor_tensor(
-                        out=pt[:, t, cols],
-                        in0=acc[:, cols],
-                        scalar=rstd[:, t, h : h + 1],
-                        in1=ta[:, t, :],
-                        op0=ALU.mult,
-                        op1=ALU.mult,
-                    )
-                    nc.vector.scalar_tensor_tensor(
-                        out=qt[:, t, cols].rearrange("p (j e) -> p j e", e=2),
-                        in0=acc[:, cols].rearrange("p (j e) -> p j e", e=2)[:, :, ::-1],
-                        scalar=rstd[:, t, h : h + 1],
-                        in1=tb[:, t, :].rearrange("p (j e) -> p j e", e=2),
-                        op0=ALU.mult,
-                        op1=ALU.mult,
-                    )
-            if b == QK_BLOCKS - 1:
-                for t in range(0, TPG, 2):
-                    nc.vector.tensor_tensor(
-                        out=pt[:, t : t + 2, :], in0=pt[:, t : t + 2, :], in1=qt[:, t : t + 2, :], op=ALU.add
-                    )
-                    nc.sync.dma_start(out=out_block(b)[:, t : t + 2, :], in_=pt[:, t : t + 2, :])
-                return
-            nc.gpsimd.tensor_tensor(
-                out=pt[:].rearrange("p t n -> p (t n)"),
-                in0=pt[:].rearrange("p t n -> p (t n)"),
-                in1=qt[:].rearrange("p t n -> p (t n)"),
-                op=ALU.add,
-            )
-            if wide:
-                nc.scalar.activation(
-                    out=rstd[:].rearrange("p t h -> p (t h)"),
-                    in_=ms[:].rearrange("p t h -> p (t h)"),
-                    func=ACT.Abs_reciprocal_sqrt,
-                    bias=eps_t[:],
-                )
-                for t in range(TPG):
-                    for h in range(HEADS_PER_BLK):
-                        jobs.append((b, pt, rstd, t, h))
-                return
-            nc.sync.dma_start(out=out_block(b), in_=pt[:])
+                second_half()
+                waiting.append((b, t, acc, ms, rstd, pt, qt))
 
         v_done = 0
         with tc.manual_schedule():
             for b in range(QK_BLOCKS):
                 qk_block(b)
-                if b % 2 == 1:
-                    v_bank(v_done, b)
+                if b % V_BLOCK in V_AFTER:
+                    v_bank(v_done)
                     v_done += 1
-                if b % 2 == 1 and b < 8:
-                    table_step(nc.gpsimd, 2, (b // 2) // 2, (b // 2) % 2)
             for i in range(v_done, TOKEN_TILES):
-                v_bank(i, QK_BLOCKS + SCALE_LAG)
+                v_bank(i)

@@ -30,8 +30,6 @@ W_PLANE_RANGES = ((0, 1), (1, 3), (3, 6))
 X_PLANE_RANGES = ((0, 1), (1, 6))
 WARM_BEFORE = 10
 WARM_AFTER = 2
-QK_BLOCKS = GROUPS * V_BLOCK
-V_AFTER = (1, 3, 4)
 
 FLOPS = 2 * TOKENS * D_IN * 3072
 
@@ -42,11 +40,8 @@ def tile_attention_pa_kernel(
     nc = tc.nc
     with ExitStack() as ctx:
         keep = ctx.enter_context(tc.tile_pool(name="keep", bufs=1))
-        pt_pool = ctx.enter_context(tc.tile_pool(name="pt_pool", bufs=6))
-        qt_pool = ctx.enter_context(tc.tile_pool(name="qt_pool", bufs=4))
-        vt_pool = ctx.enter_context(tc.tile_pool(name="vt_pool", bufs=10))
-        stats = ctx.enter_context(tc.tile_pool(name="stats", bufs=4))
-        junk_pool = ctx.enter_context(tc.tile_pool(name="junk_pool", bufs=8))
+        work = ctx.enter_context(tc.tile_pool(name="work", bufs=4))
+        small = ctx.enter_context(tc.tile_pool(name="small", bufs=8))
         psum = ctx.enter_context(tc.psum_pool(name="psum", bufs=8))
 
         ones = keep.tile([P, P], BF16, name="ones")
@@ -63,19 +58,19 @@ def tile_attention_pa_kernel(
         xc = []
         wc = []
         for c in range(GROUPS):
-            xc_t = keep.tile([P, PASSES, 2 * NBLK], U8, name="xc%d" % c, align_bytes=64)
-            xc.append(xc_t)
+            xc_t = keep.tile([P, PASSES * 2 * NBLK + 256], U8, name="xc%d" % c, align_bytes=256)
+            xc.append(xc_t[:, 128 : 128 + PASSES * 2 * NBLK].rearrange("p (g n) -> p g n", g=PASSES))
         for n in range(BLOCKS):
-            wc_t = keep.tile([P, PASSES, 2 * NBLK], U8, name="wc%d" % n, align_bytes=64)
-            wc.append(wc_t)
+            wc_t = keep.tile([P, PASSES * 2 * NBLK + 256], U8, name="wc%d" % n, align_bytes=256)
+            wc.append(wc_t[:, 0 : PASSES * 2 * NBLK].rearrange("p (g n) -> p g n", g=PASSES))
         xs = []
         ws = []
         for i, (lo, hi) in enumerate(X_PLANE_RANGES):
-            xs_t = keep.tile([P, PASSES, (hi - lo) * NBLK], U8, name="xs%d" % i, align_bytes=64)
-            xs.append(xs_t)
+            xs_t = keep.tile([P, PASSES * (hi - lo) * NBLK + 256], U8, name="xs%d" % i, align_bytes=256)
+            xs.append(xs_t[:, 192 : 192 + PASSES * (hi - lo) * NBLK].rearrange("p (g n) -> p g n", g=PASSES))
         for i, (lo, hi) in enumerate(W_PLANE_RANGES):
-            ws_t = keep.tile([P, PASSES, (hi - lo) * NBLK], U8, name="ws%d" % i, align_bytes=64)
-            ws.append(ws_t)
+            ws_t = keep.tile([P, PASSES * (hi - lo) * NBLK + 256], U8, name="ws%d" % i, align_bytes=256)
+            ws.append(ws_t[:, 64 : 64 + PASSES * (hi - lo) * NBLK].rearrange("p (g n) -> p g n", g=PASSES))
 
         eps_t = keep.tile([P, 1], F32, name="eps_t")
         for plane in (xs[0], ws[0]):
@@ -113,10 +108,10 @@ def tile_attention_pa_kernel(
         load_codes(wc[1], wqkv_words, 1)
         load_scales(ws[1], wqkv_scales, W_PLANE_RANGES[1], range(4))
         load_codes(wc[2], wqkv_words, 2)
-        load_scales(ws[2], wqkv_scales, W_PLANE_RANGES[2], range(4))
-        load_codes(wc[5], wqkv_words, 5)
         load_codes(wc[3], wqkv_words, 3)
+        load_scales(ws[2], wqkv_scales, W_PLANE_RANGES[2], range(4))
         load_codes(wc[4], wqkv_words, 4)
+        load_codes(wc[5], wqkv_words, 5)
         load_scales(xs[1], x_scales, X_PLANE_RANGES[1], range(4))
         for c in range(1, GROUPS):
             load_codes(xc[c], x_words, c)
@@ -149,33 +144,31 @@ def tile_attention_pa_kernel(
         tabs = {}
         full = [P, TPG, HD // 2, 2]
 
-        def table_step(eng, m, ki, part):
+        def build_tables(eng, m):
             pairs = fc[:, TPG * m : TPG * (m + 1), :].rearrange("p t (j e) -> p t j e", e=2)
-            tab = keep.tile([P, TPG, HD], F32, name="tab_%d_%d_%d" % (m, ki, part))
-            gains = w_all if part == 0 else w_swp
-            eng.tensor_tensor(
-                out=tab[:].rearrange("p t (j e) -> p t j e", e=2),
-                in0=pairs[:, :, :, part : part + 1].to_broadcast(full),
-                in1=gains[:, ki : ki + 1, :, :].to_broadcast(full),
-                op=ALU.mult,
-            )
-            tabs[(m, ki, part)] = tab
+            for ki, key in enumerate(("q", "k")):
+                ta = keep.tile([P, TPG, HD], F32, name="ta_%s%d" % (key, m))
+                tb = keep.tile([P, TPG, HD], F32, name="tb_%s%d" % (key, m))
+                eng.tensor_tensor(
+                    out=ta[:].rearrange("p t (j e) -> p t j e", e=2),
+                    in0=pairs[:, :, :, 0:1].to_broadcast(full),
+                    in1=w_all[:, ki : ki + 1, :, :].to_broadcast(full),
+                    op=ALU.mult,
+                )
+                eng.tensor_tensor(
+                    out=tb[:].rearrange("p t (j e) -> p t j e", e=2),
+                    in0=pairs[:, :, :, 1:2].to_broadcast(full),
+                    in1=w_swp[:, ki : ki + 1, :, :].to_broadcast(full),
+                    op=ALU.mult,
+                )
+                tabs[(key, m)] = (ta, tb)
 
-        for m, eng in ((0, nc.vector), (1, nc.gpsimd)):
-            for ki in range(2):
-                for part in range(2):
-                    table_step(eng, m, ki, part)
+        build_tables(nc.vector, 0)
+        build_tables(nc.gpsimd, 1)
 
         out_q = out_0.rearrange("b s h d -> (b s) (h d)").rearrange("(c t p) n -> c p t n", t=TPG, p=P)
         out_k = out_1.rearrange("b s h d -> (b s) (h d)").rearrange("(c t p) n -> c p t n", t=TPG, p=P)
         out_v = out_2.rearrange("b s h d -> (b s) (h d)").rearrange("(i p) n -> i p n", p=P)
-
-        def out_block(b):
-            c = b // V_BLOCK
-            n = b % V_BLOCK
-            if n == K_BLOCK:
-                return out_k[c]
-            return out_q[c][:, :, n * NBLK : (n + 1) * NBLK]
 
         def project(c, t, n):
             acc = psum.tile([P, NBLK], F32, name="acc")
@@ -191,91 +184,119 @@ def tile_attention_pa_kernel(
                 )
             return acc
 
-        waiting = []
+        def v_bank(i):
+            acc = project(i // TPG, i % TPG, V_BLOCK)
+            vt = work.tile([P, NBLK], F32, name="vt", bufs=10)
+            nc.scalar.copy(out=vt[:], in_=acc[:])
+            nc.sync.dma_start(out=out_v[i], in_=vt[:])
 
-        def second_half():
-            if len(waiting) == 0:
-                return
-            b, t, acc, ms, rstd, pt, qt = waiting[0]
-            waiting.clear()
-            ki = 1 if b % V_BLOCK == K_BLOCK else 0
-            ta = tabs[((b // V_BLOCK) % POS_GROUPS, ki, 0)]
-            tb = tabs[((b // V_BLOCK) % POS_GROUPS, ki, 1)]
-            nc.scalar.activation(
-                out=rstd[:, t, :], in_=ms[:, t, :], func=ACT.Abs_reciprocal_sqrt, bias=eps_t[:]
-            )
-            for h in range(HEADS_PER_BLK):
-                cols = slice(h * HD, (h + 1) * HD)
-                nc.vector.scalar_tensor_tensor(
-                    out=pt[:, t, cols],
-                    in0=acc[:, cols],
-                    scalar=rstd[:, t, h : h + 1],
-                    in1=ta[:, t, :],
-                    op0=ALU.mult,
-                    op1=ALU.mult,
-                )
-                nc.vector.scalar_tensor_tensor(
-                    out=qt[:, t, cols].rearrange("p (j e) -> p j e", e=2),
-                    in0=acc[:, cols].rearrange("p (j e) -> p j e", e=2)[:, :, ::-1],
-                    scalar=rstd[:, t, h : h + 1],
-                    in1=tb[:, t, :].rearrange("p (j e) -> p j e", e=2),
-                    op0=ALU.mult,
-                    op1=ALU.mult,
-                )
-            if t < TPG - 1:
-                return
-            if b == QK_BLOCKS - 1:
-                for half in range(0, TPG, 2):
-                    nc.vector.tensor_tensor(
-                        out=pt[:, half : half + 2, :],
-                        in0=pt[:, half : half + 2, :],
-                        in1=qt[:, half : half + 2, :],
-                        op=ALU.add,
+        def out_block(c, n):
+            if n == K_BLOCK:
+                return out_k[c]
+            return out_q[c][:, :, n * NBLK : (n + 1) * NBLK]
+
+        def qk_block(c, n, wide, last):
+            pt = work.tile([P, TPG, NBLK], F32, name="pt", bufs=6)
+            qt = work.tile([P, TPG, NBLK], F32, name="qt")
+            ta, tb = tabs[("k" if n == K_BLOCK else "q", c % POS_GROUPS)]
+            rstd = small.tile([P, TPG, HEADS_PER_BLK], F32, name="rstd")
+            by_head = [P, HEADS_PER_BLK, HD // 2, 2]
+            for t in range(TPG):
+                acc = project(c, t, n)
+                ms = small.tile([P, HEADS_PER_BLK], F32, name="ms")
+                for h in range(HEADS_PER_BLK):
+                    junk = small.tile([P, HD], BF16, name="junk", bufs=2)
+                    nc.scalar.activation(
+                        out=junk[:],
+                        in_=acc[:, h * HD : (h + 1) * HD],
+                        func=ACT.Square,
+                        scale=INV_SQRT_HD,
+                        accum_out=ms[:, h : h + 1],
                     )
-                    nc.sync.dma_start(out=out_block(b)[:, half : half + 2, :], in_=pt[:, half : half + 2, :])
-                return
+                nc.scalar.activation(
+                    out=rstd[:, t, :], in_=ms[:], func=ACT.Abs_reciprocal_sqrt, bias=eps_t[:]
+                )
+                if wide:
+                    acc4 = acc[:].rearrange("p (h j e) -> p h j e", h=HEADS_PER_BLK, e=2)
+                    nc.vector.tensor_tensor(
+                        out=pt[:, t, :].rearrange("p (h j e) -> p h j e", h=HEADS_PER_BLK, e=2),
+                        in0=acc4,
+                        in1=ta[:, t : t + 1, :].rearrange("p o (j e) -> p o j e", e=2).to_broadcast(by_head),
+                        op=ALU.mult,
+                    )
+                    nc.vector.tensor_tensor(
+                        out=qt[:, t, :].rearrange("p (h j e) -> p h j e", h=HEADS_PER_BLK, e=2),
+                        in0=acc4[:, :, :, ::-1],
+                        in1=tb[:, t : t + 1, :].rearrange("p o (j e) -> p o j e", e=2).to_broadcast(by_head),
+                        op=ALU.mult,
+                    )
+                    continue
+                for h in range(HEADS_PER_BLK):
+                    cols = slice(h * HD, (h + 1) * HD)
+                    nc.vector.scalar_tensor_tensor(
+                        out=pt[:, t, cols],
+                        in0=acc[:, cols],
+                        scalar=rstd[:, t, h : h + 1],
+                        in1=ta[:, t, :],
+                        op0=ALU.mult,
+                        op1=ALU.mult,
+                    )
+                    nc.vector.scalar_tensor_tensor(
+                        out=qt[:, t, cols].rearrange("p (j e) -> p j e", e=2),
+                        in0=acc[:, cols].rearrange("p (j e) -> p j e", e=2)[:, :, ::-1],
+                        scalar=rstd[:, t, h : h + 1],
+                        in1=tb[:, t, :].rearrange("p (j e) -> p j e", e=2),
+                        op0=ALU.mult,
+                        op1=ALU.mult,
+                    )
+            if last:
+                for t in range(0, TPG, 2):
+                    nc.vector.tensor_tensor(
+                        out=pt[:, t : t + 2, :], in0=pt[:, t : t + 2, :], in1=qt[:, t : t + 2, :], op=ALU.add
+                    )
+                    nc.sync.dma_start(out=out_block(c, n)[:, t : t + 2, :], in_=pt[:, t : t + 2, :])
+                return None
             nc.gpsimd.tensor_tensor(
                 out=pt[:].rearrange("p t n -> p (t n)"),
                 in0=pt[:].rearrange("p t n -> p (t n)"),
                 in1=qt[:].rearrange("p t n -> p (t n)"),
                 op=ALU.add,
             )
-            nc.sync.dma_start(out=out_block(b), in_=pt[:])
-            if b % 2 == 1 and b < 8:
-                table_step(nc.gpsimd, 2, (b // 2) // 2, (b // 2) % 2)
+            if wide:
+                return (pt, rstd, c, n)
+            nc.sync.dma_start(out=out_block(c, n), in_=pt[:])
+            return None
 
-        def v_bank(i):
-            acc = project(i // TPG, i % TPG, V_BLOCK)
-            vt = vt_pool.tile([P, NBLK], F32, name="vt")
-            nc.scalar.copy(out=vt[:], in_=acc[:])
-            nc.sync.dma_start(out=out_v[i], in_=vt[:])
-            second_half()
-
-        def qk_block(b):
-            pt = pt_pool.tile([P, TPG, NBLK], F32, name="pt")
-            qt = qt_pool.tile([P, TPG, NBLK], F32, name="qt")
-            ms = stats.tile([P, TPG, HEADS_PER_BLK], F32, name="ms")
-            rstd = stats.tile([P, TPG, HEADS_PER_BLK], F32, name="rstd")
+        def finish_wide(todo):
+            pt, rstd, c, n = todo
             for t in range(TPG):
-                acc = project(b // V_BLOCK, t, b % V_BLOCK)
                 for h in range(HEADS_PER_BLK):
-                    junk = junk_pool.tile([P, HD], BF16, name="junk")
+                    cols = slice(h * HD, (h + 1) * HD)
                     nc.scalar.activation(
-                        out=junk[:],
-                        in_=acc[:, h * HD : (h + 1) * HD],
-                        func=ACT.Square,
-                        scale=INV_SQRT_HD,
-                        accum_out=ms[:, t, h : h + 1],
+                        out=pt[:, t, cols], in_=pt[:, t, cols], func=ACT.Copy, scale=rstd[:, t, h : h + 1]
                     )
-                second_half()
-                waiting.append((b, t, acc, ms, rstd, pt, qt))
+            nc.sync.dma_start(out=out_block(c, n), in_=pt[:])
 
         v_done = 0
-        with tc.manual_schedule():
-            for b in range(QK_BLOCKS):
-                qk_block(b)
-                if b % V_BLOCK in V_AFTER:
-                    v_bank(v_done)
-                    v_done += 1
-            for i in range(v_done, TOKEN_TILES):
-                v_bank(i)
+        waiting = []
+        finished = 0
+        n_blocks = GROUPS * V_BLOCK
+        for b in range(n_blocks):
+            c = b // V_BLOCK
+            n = b % V_BLOCK
+            todo = qk_block(c, n, False, b == n_blocks - 1)
+            if todo is not None:
+                waiting.append(todo)
+            if finished < len(waiting) and waiting[finished][2] * V_BLOCK + waiting[finished][3] <= b - 2:
+                finish_wide(waiting[finished])
+                finished += 1
+            if b % 2 == 1:
+                v_bank(v_done)
+                v_done += 1
+            if b == 1:
+                build_tables(nc.gpsimd, 2)
+        for i in range(v_done, TOKEN_TILES):
+            v_bank(i)
+            if finished < len(waiting):
+                finish_wide(waiting[finished])
+                finished += 1

@@ -30,6 +30,7 @@ W_PLANE_RANGES = ((0, 1), (1, 3), (3, 6))
 X_PLANE_RANGES = ((0, 1), (1, 6))
 WARM_BEFORE = 10
 WARM_AFTER = 2
+V_FIRST = 4
 
 FLOPS = 2 * TOKENS * D_IN * 3072
 
@@ -290,7 +291,7 @@ def tile_attention_pa_kernel(
             if finished < len(waiting) and waiting[finished][2] * V_BLOCK + waiting[finished][3] <= b - 2:
                 finish_wide(waiting[finished])
                 finished += 1
-            if b % 2 == 1:
+            if b >= V_FIRST and b % 3 != 2:
                 v_bank(v_done)
                 v_done += 1
             if b == 1:

@@ -48,12 +48,11 @@ def tile_attention_pa_kernel(
         ones = keep.tile([P, P], BF16, name="ones")
         idle_rhs = keep.tile([P, NBLK], BF16, name="idle_rhs")
         w_rows = keep.tile([P, 2 * HD], BF16, name="w_rows")
-        nc.gpsimd.memset(w_rows[:], 0.0)
-        nc.gpsimd.dma_start(out=w_rows[0:1, 0:HD], in_=q_norm_w.rearrange("(o d) -> o d", o=1))
-        nc.gpsimd.dma_start(out=w_rows[0:1, HD : 2 * HD], in_=k_norm_w.rearrange("(o d) -> o d", o=1))
+        nc.vector.memset(w_rows[:], 0.0)
+        nc.sync.dma_start(out=w_rows[0:1, 0:HD], in_=q_norm_w.rearrange("(o d) -> o d", o=1))
+        nc.sync.dma_start(out=w_rows[0:1, HD : 2 * HD], in_=k_norm_w.rearrange("(o d) -> o d", o=1))
         fc = keep.tile([P, 12, HD], BF16, name="fc")
         fc_view = freqs_cis.rearrange("(t p) j e -> p t (j e)", p=P)
-        nc.gpsimd.dma_start(out=fc[:, 0:4, :], in_=fc_view[:, 0:4, :])
         nc.gpsimd.dma_start(out=fc[:, 4:12, :], in_=fc_view[:, 4:12, :])
 
         xc = []
@@ -104,6 +103,7 @@ def tile_attention_pa_kernel(
         load_scales(xs[0], x_scales, X_PLANE_RANGES[0], (0, 1))
         load_codes(xc[0], x_words, 0)
         load_codes(wc[0], wqkv_words, 0)
+        nc.sync.dma_start(out=fc[:, 0:4, :], in_=fc_view[:, 0:4, :])
         load_scales(xs[0], x_scales, X_PLANE_RANGES[0], (2, 3))
         load_scales(ws[0], wqkv_scales, W_PLANE_RANGES[0], range(4))
         load_codes(wc[1], wqkv_words, 1)

@@ -28,8 +28,8 @@ EPS = 1e-6
 INV_SQRT_HD = 1.0 / (128.0 ** 0.5)
 W_PLANE_RANGES = ((0, 1), (1, 3), (3, 6))
 X_PLANE_RANGES = ((0, 1), (1, 6))
-WARM_BEFORE = 10
-WARM_AFTER = 2
+WARM_BEFORE = 4
+WARM_AFTER = 3
 V_FIRST = 4
 
 FLOPS = 2 * TOKENS * D_IN * 3072
@@ -53,7 +53,6 @@ def tile_attention_pa_kernel(
         nc.sync.dma_start(out=w_rows[0:1, HD : 2 * HD], in_=k_norm_w.rearrange("(o d) -> o d", o=1))
         fc = keep.tile([P, 12, HD], BF16, name="fc")
         fc_view = freqs_cis.rearrange("(t p) j e -> p t (j e)", p=P)
-        nc.gpsimd.dma_start(out=fc[:, 4:12, :], in_=fc_view[:, 4:12, :])
 
         xc = []
         wc = []
@@ -100,19 +99,23 @@ def tile_attention_pa_kernel(
                     .bitcast(I32),
                 )
 
-        load_scales(xs[0], x_scales, X_PLANE_RANGES[0], (0, 1))
+        def load_freqs(m):
+            nc.sync.dma_start(out=fc[:, TPG * m : TPG * (m + 1), :], in_=fc_view[:, TPG * m : TPG * (m + 1), :])
+
+        load_scales(xs[0], x_scales, X_PLANE_RANGES[0], range(4))
         load_codes(xc[0], x_words, 0)
         load_codes(wc[0], wqkv_words, 0)
-        nc.sync.dma_start(out=fc[:, 0:4, :], in_=fc_view[:, 0:4, :])
-        load_scales(xs[0], x_scales, X_PLANE_RANGES[0], (2, 3))
         load_scales(ws[0], wqkv_scales, W_PLANE_RANGES[0], range(4))
+        load_freqs(0)
         load_codes(wc[1], wqkv_words, 1)
         load_scales(ws[1], wqkv_scales, W_PLANE_RANGES[1], range(4))
+        load_freqs(1)
         load_codes(wc[2], wqkv_words, 2)
         load_codes(wc[3], wqkv_words, 3)
         load_scales(ws[2], wqkv_scales, W_PLANE_RANGES[2], range(4))
         load_codes(wc[4], wqkv_words, 4)
         load_codes(wc[5], wqkv_words, 5)
+        load_freqs(2)
         load_scales(xs[1], x_scales, X_PLANE_RANGES[1], range(4))
         for c in range(1, GROUPS):
             load_codes(xc[c], x_words, c)

@@ -174,32 +174,32 @@ def tile_attention_pa_kernel(
         out_k = out_1.rearrange("b s h d -> (b s) (h d)").rearrange("(c t p) n -> c p t n", t=TPG, p=P)
         out_v = out_2.rearrange("b s h d -> (b s) (h d)").rearrange("(i p) n -> i p n", p=P)
 
-        def project(c, t, n):
+        def project(c, t, n, first_col=0, width=NBLK):
             acc = psum.tile([P, NBLK], F32, name="acc")
             for g in range(PASSES):
                 nc.tensor.matmul_mx(
-                    out=acc[:],
+                    out=acc[:, 0:width],
                     lhsT=xc[c][:, g, t * 2 * P : (t + 1) * 2 * P].bitcast(FP4X4),
                     lhsT_scale=plane_cols(xs, X_PLANE_RANGES, c, g, t * P, P),
-                    rhs=wc[n][:, g, :].bitcast(FP4X4),
-                    rhs_scale=plane_cols(ws, W_PLANE_RANGES, n, g, 0, NBLK),
+                    rhs=wc[n][:, g, 2 * first_col : 2 * (first_col + width)].bitcast(FP4X4),
+                    rhs_scale=plane_cols(ws, W_PLANE_RANGES, n, g, first_col, width),
                     start=(g == 0),
                     stop=(g == PASSES - 1),
                 )
             return acc
 
-        def v_bank(i):
-            acc = project(i // TPG, i % TPG, V_BLOCK)
+        def v_bank(i, first_col=0, width=NBLK):
+            acc = project(i // TPG, i % TPG, V_BLOCK, first_col, width)
             vt = work.tile([P, NBLK], F32, name="vt", bufs=10)
-            nc.scalar.copy(out=vt[:], in_=acc[:])
-            nc.sync.dma_start(out=out_v[i], in_=vt[:])
+            nc.scalar.copy(out=vt[:, 0:width], in_=acc[:, 0:width])
+            nc.sync.dma_start(out=out_v[i][:, first_col : first_col + width], in_=vt[:, 0:width])
 
         def out_block(c, n):
             if n == K_BLOCK:
                 return out_k[c]
             return out_q[c][:, :, n * NBLK : (n + 1) * NBLK]
 
-        def qk_block(c, n, wide, last):
+        def qk_block(c, n, wide, last, halves_on=None):
             pt = work.tile([P, TPG, NBLK], F32, name="pt", bufs=6)
             qt = work.tile([P, TPG, NBLK], F32, name="qt")
             ta, tb = tabs[("k" if n == K_BLOCK else "q", c % POS_GROUPS)]
@@ -253,6 +253,16 @@ def tile_attention_pa_kernel(
                         op0=ALU.mult,
                         op1=ALU.mult,
                     )
+                if halves_on is not None and t % 2 == 1:
+                    halves_on.tensor_tensor(
+                        out=pt[:, t - 1 : t + 1, :].rearrange("p t n -> p (t n)"),
+                        in0=pt[:, t - 1 : t + 1, :].rearrange("p t n -> p (t n)"),
+                        in1=qt[:, t - 1 : t + 1, :].rearrange("p t n -> p (t n)"),
+                        op=ALU.add,
+                    )
+                    nc.sync.dma_start(out=out_block(c, n)[:, t - 1 : t + 1, :], in_=pt[:, t - 1 : t + 1, :])
+            if halves_on is not None:
+                return None
             if last:
                 for t in range(0, TPG, 2):
                     nc.vector.tensor_tensor(
@@ -288,7 +298,7 @@ def tile_attention_pa_kernel(
         for b in range(n_blocks):
             c = b // V_BLOCK
             n = b % V_BLOCK
-            todo = qk_block(c, n, False, b == n_blocks - 1)
+            todo = qk_block(c, n, False, False, {n_blocks - 2: nc.gpsimd, n_blocks - 1: nc.vector}.get(b))
             if todo is not None:
                 waiting.append(todo)
             if finished < len(waiting) and waiting[finished][2] * V_BLOCK + waiting[finished][3] <= b - 2:
@@ -299,8 +309,7 @@ def tile_attention_pa_kernel(
                 v_done += 1
             if b == 1:
                 build_tables(nc.gpsimd, 2)
-        for i in range(v_done, TOKEN_TILES):
+        for i in range(v_done, TOKEN_TILES - 1):
             v_bank(i)
-            if finished < len(waiting):
-                finish_wide(waiting[finished])
-                finished += 1
+        for first_col in range(0, NBLK, NBLK // 2):
+            v_bank(TOKEN_TILES - 1, first_col, NBLK // 2)

@@ -188,11 +188,11 @@ def tile_attention_pa_kernel(
                 )
             return acc
 
-        def v_bank(i, first_col=0, width=NBLK):
+        def v_bank(i, first_col=0, width=NBLK, queue=nc.sync):
             acc = project(i // TPG, i % TPG, V_BLOCK, first_col, width)
             vt = work.tile([P, NBLK], F32, name="vt", bufs=10)
             nc.scalar.copy(out=vt[:, 0:width], in_=acc[:, 0:width])
-            nc.sync.dma_start(out=out_v[i][:, first_col : first_col + width], in_=vt[:, 0:width])
+            queue.dma_start(out=out_v[i][:, first_col : first_col + width], in_=vt[:, 0:width])
 
         def out_block(c, n):
             if n == K_BLOCK:
@@ -310,6 +310,6 @@ def tile_attention_pa_kernel(
             if b == 1:
                 build_tables(nc.gpsimd, 2)
         for i in range(v_done, TOKEN_TILES - 1):
-            v_bank(i)
+            v_bank(i, queue=nc.scalar)
         for first_col in range(0, NBLK, NBLK // 2):
-            v_bank(TOKEN_TILES - 1, first_col, NBLK // 2)
+            v_bank(TOKEN_TILES - 1, first_col, NBLK // 2, queue=nc.scalar)

from contextlib import ExitStack

import concourse.mybir as mybir

F32 = mybir.dt.float32
BF16 = mybir.dt.bfloat16
U8 = mybir.dt.uint8
I32 = mybir.dt.int32
FP4X4 = mybir.dt.float4_e2m1fn_x4
ACT = mybir.ActivationFunctionType
ALU = mybir.AluOpType

P = 128
TOKENS = 3072
D_IN = 2048
PASSES = D_IN // 512
HD = 128
NBLK = 512
HEADS_PER_BLK = NBLK // HD
K_BLOCK = 4
V_BLOCK = 5
BLOCKS = 6
TPG = 4
GROUPS = TOKENS // (TPG * P)
TOKEN_TILES = TOKENS // P
POS_GROUPS = 3
EPS = 1e-6
INV_SQRT_HD = 1.0 / (128.0 ** 0.5)
W_PLANE_RANGES = ((0, 1), (1, 3), (3, 6))
X_PLANE_RANGES = ((0, 1), (1, 6))
WARM_BEFORE = 4
WARM_AFTER = 3
V_FIRST = 4

FLOPS = 2 * TOKENS * D_IN * 3072


def tile_attention_pa_kernel(
    tc, x_words, x_scales, freqs_cis, wqkv_words, wqkv_scales, q_norm_w, k_norm_w, out_0, out_1, out_2
):
    nc = tc.nc
    with ExitStack() as ctx:
        keep = ctx.enter_context(tc.tile_pool(name="keep", bufs=1))
        work = ctx.enter_context(tc.tile_pool(name="work", bufs=4))
        small = ctx.enter_context(tc.tile_pool(name="small", bufs=8))
        psum = ctx.enter_context(tc.psum_pool(name="psum", bufs=8))

        ones = keep.tile([P, P], BF16, name="ones")
        idle_rhs = keep.tile([P, NBLK], BF16, name="idle_rhs")
        w_rows = keep.tile([P, 2 * HD], BF16, name="w_rows")
        nc.vector.memset(w_rows[:], 0.0)
        nc.sync.dma_start(out=w_rows[0:1, 0:HD], in_=q_norm_w.rearrange("(o d) -> o d", o=1))
        nc.sync.dma_start(out=w_rows[0:1, HD : 2 * HD], in_=k_norm_w.rearrange("(o d) -> o d", o=1))
        fc = keep.tile([P, 12, HD], BF16, name="fc")
        fc_view = freqs_cis.rearrange("(t p) j e -> p t (j e)", p=P)

        xc = []
        wc = []
        for c in range(GROUPS):
            xc_t = keep.tile([P, PASSES * 2 * NBLK + 256], U8, name="xc%d" % c, align_bytes=256)
            xc.append(xc_t[:, 128 : 128 + PASSES * 2 * NBLK].rearrange("p (g n) -> p g n", g=PASSES))
        for n in range(BLOCKS):
            wc_t = keep.tile([P, PASSES * 2 * NBLK + 256], U8, name="wc%d" % n, align_bytes=256)
            wc.append(wc_t[:, 0 : PASSES * 2 * NBLK].rearrange("p (g n) -> p g n", g=PASSES))
        xs = []
        ws = []
        for i, (lo, hi) in enumerate(X_PLANE_RANGES):
            xs_t = keep.tile([P, PASSES * (hi - lo) * NBLK + 256], U8, name="xs%d" % i, align_bytes=256)
            xs.append(xs_t[:, 192 : 192 + PASSES * (hi - lo) * NBLK].rearrange("p (g n) -> p g n", g=PASSES))
        for i, (lo, hi) in enumerate(W_PLANE_RANGES):
            ws_t = keep.tile([P, PASSES * (hi - lo) * NBLK + 256], U8, name="ws%d" % i, align_bytes=256)
            ws.append(ws_t[:, 64 : 64 + PASSES * (hi - lo) * NBLK].rearrange("p (g n) -> p g n", g=PASSES))

        eps_t = keep.tile([P, 1], F32, name="eps_t")
        for plane in (xs[0], ws[0]):
            nc.vector.memset(plane[:].rearrange("p g n -> p (g n)").bitcast(I32), 0)
        nc.vector.memset(ones[:], 1.0)
        nc.vector.memset(idle_rhs[:], 0.0)
        nc.vector.memset(eps_t[:], EPS)
        for plane in (ws[1], ws[2], xs[1]):
            nc.vector.memset(plane[:].rearrange("p g n -> p (g n)").bitcast(I32), 0)

        warm = keep.tile([P, 1], F32, name="warm")
        nc.scalar.activation(out=warm[:], in_=eps_t[:], func=ACT.Abs_reciprocal_sqrt)

        def load_codes(dst, src, c):
            nc.sync.dma_start(
                out=dst[:].bitcast(I32),
                in_=src[:, :, c * 2 * NBLK : (c + 1) * 2 * NBLK].rearrange("g p n -> p g n").bitcast(I32),
            )

        def load_scales(dst, src, blocks, quads):
            lo, hi = blocks
            for quad in quads:
                nc.sync.dma_start(
                    out=dst[32 * quad : 32 * quad + 4, :, :].bitcast(I32),
                    in_=src[:, 4 * quad : 4 * quad + 4, lo * NBLK : hi * NBLK]
                    .rearrange("g r n -> r g n")
                    .bitcast(I32),
                )

        def load_freqs(m):
            nc.sync.dma_start(out=fc[:, TPG * m : TPG * (m + 1), :], in_=fc_view[:, TPG * m : TPG * (m + 1), :])

        load_scales(xs[0], x_scales, X_PLANE_RANGES[0], range(4))
        load_codes(xc[0], x_words, 0)
        load_codes(wc[0], wqkv_words, 0)
        load_scales(ws[0], wqkv_scales, W_PLANE_RANGES[0], range(4))
        load_freqs(0)
        load_codes(wc[1], wqkv_words, 1)
        load_scales(ws[1], wqkv_scales, W_PLANE_RANGES[1], range(4))
        load_freqs(1)
        load_codes(wc[2], wqkv_words, 2)
        load_codes(wc[3], wqkv_words, 3)
        load_scales(ws[2], wqkv_scales, W_PLANE_RANGES[2], range(4))
        load_codes(wc[4], wqkv_words, 4)
        load_codes(wc[5], wqkv_words, 5)
        load_freqs(2)
        load_scales(xs[1], x_scales, X_PLANE_RANGES[1], range(4))
        for c in range(1, GROUPS):
            load_codes(xc[c], x_words, c)

        def plane_cols(planes, ranges, blk, g, first_col, width):
            for tile_i, (lo, hi) in enumerate(ranges):
                if lo <= blk < hi:
                    start = (blk - lo) * NBLK + first_col
                    return planes[tile_i][:, g, start : start + width]
            return None

        idle_ps = psum.tile([P, NBLK], F32, name="acc")
        for i in range(WARM_BEFORE):
            nc.tensor.matmul(out=idle_ps[:], lhsT=ones[:], rhs=idle_rhs[:], start=True, stop=True)
        w_ps = psum.tile([P, NBLK], F32, name="acc")
        nc.tensor.matmul(out=w_ps[:, 0 : 2 * HD], lhsT=ones[:], rhs=w_rows[:], start=True, stop=True)
        idle_ps2 = psum.tile([P, NBLK], F32, name="acc")
        for i in range(WARM_AFTER):
            nc.tensor.matmul(out=idle_ps2[:], lhsT=ones[:], rhs=idle_rhs[:], start=True, stop=True)

        w_all = keep.tile([P, 2, HD // 2, 2], F32, name="w_all")
        w_swp = keep.tile([P, 2, HD // 2, 2], F32, name="w_swp")
        w_ps_v = w_ps[:, 0 : 2 * HD].rearrange("p (k j e) -> p k j e", k=2, e=2)
        nc.vector.tensor_copy(out=w_all[:], in_=w_ps_v)
        nc.vector.tensor_scalar(
            out=w_swp[:, :, :, 0:1], in0=w_ps_v[:, :, :, 1:2], scalar1=-1.0, scalar2=None, op0=ALU.mult
        )
        nc.vector.tensor_copy(out=w_swp[:, :, :, 1:2], in_=w_ps_v[:, :, :, 0:1])

        tabs = {}
        full = [P, TPG, HD // 2, 2]

        def build_tables(eng, m):
            pairs = fc[:, TPG * m : TPG * (m + 1), :].rearrange("p t (j e) -> p t j e", e=2)
            for ki, key in enumerate(("q", "k")):
                ta = keep.tile([P, TPG, HD], F32, name="ta_%s%d" % (key, m))
                tb = keep.tile([P, TPG, HD], F32, name="tb_%s%d" % (key, m))
                eng.tensor_tensor(
                    out=ta[:].rearrange("p t (j e) -> p t j e", e=2),
                    in0=pairs[:, :, :, 0:1].to_broadcast(full),
                    in1=w_all[:, ki : ki + 1, :, :].to_broadcast(full),
                    op=ALU.mult,
                )
                eng.tensor_tensor(
                    out=tb[:].rearrange("p t (j e) -> p t j e", e=2),
                    in0=pairs[:, :, :, 1:2].to_broadcast(full),
                    in1=w_swp[:, ki : ki + 1, :, :].to_broadcast(full),
                    op=ALU.mult,
                )
                tabs[(key, m)] = (ta, tb)

        build_tables(nc.vector, 0)
        build_tables(nc.gpsimd, 1)

        out_q = out_0.rearrange("b s h d -> (b s) (h d)").rearrange("(c t p) n -> c p t n", t=TPG, p=P)
        out_k = out_1.rearrange("b s h d -> (b s) (h d)").rearrange("(c t p) n -> c p t n", t=TPG, p=P)
        out_v = out_2.rearrange("b s h d -> (b s) (h d)").rearrange("(i p) n -> i p n", p=P)

        def project(c, t, n, first_col=0, width=NBLK):
            acc = psum.tile([P, NBLK], F32, name="acc")
            for g in range(PASSES):
                nc.tensor.matmul_mx(
                    out=acc[:, 0:width],
                    lhsT=xc[c][:, g, t * 2 * P : (t + 1) * 2 * P].bitcast(FP4X4),
                    lhsT_scale=plane_cols(xs, X_PLANE_RANGES, c, g, t * P, P),
                    rhs=wc[n][:, g, 2 * first_col : 2 * (first_col + width)].bitcast(FP4X4),
                    rhs_scale=plane_cols(ws, W_PLANE_RANGES, n, g, first_col, width),
                    start=(g == 0),
                    stop=(g == PASSES - 1),
                )
            return acc

        def v_bank(i, first_col=0, width=NBLK, queue=nc.sync):
            acc = project(i // TPG, i % TPG, V_BLOCK, first_col, width)
            vt = work.tile([P, NBLK], F32, name="vt", bufs=10)
            nc.scalar.copy(out=vt[:, 0:width], in_=acc[:, 0:width])
            queue.dma_start(out=out_v[i][:, first_col : first_col + width], in_=vt[:, 0:width])

        def out_block(c, n):
            if n == K_BLOCK:
                return out_k[c]
            return out_q[c][:, :, n * NBLK : (n + 1) * NBLK]

        def qk_block(c, n, wide, last, halves_on=None):
            pt = work.tile([P, TPG, NBLK], F32, name="pt", bufs=6)
            qt = work.tile([P, TPG, NBLK], F32, name="qt")
            ta, tb = tabs[("k" if n == K_BLOCK else "q", c % POS_GROUPS)]
            rstd = small.tile([P, TPG, HEADS_PER_BLK], F32, name="rstd")
            by_head = [P, HEADS_PER_BLK, HD // 2, 2]
            for t in range(TPG):
                acc = project(c, t, n)
                ms = small.tile([P, HEADS_PER_BLK], F32, name="ms")
                for h in range(HEADS_PER_BLK):
                    junk = small.tile([P, HD], BF16, name="junk", bufs=2)
                    nc.scalar.activation(
                        out=junk[:],
                        in_=acc[:, h * HD : (h + 1) * HD],
                        func=ACT.Square,
                        scale=INV_SQRT_HD,
                        accum_out=ms[:, h : h + 1],
                    )
                nc.scalar.activation(
                    out=rstd[:, t, :], in_=ms[:], func=ACT.Abs_reciprocal_sqrt, bias=eps_t[:]
                )
                if wide:
                    acc4 = acc[:].rearrange("p (h j e) -> p h j e", h=HEADS_PER_BLK, e=2)
                    nc.vector.tensor_tensor(
                        out=pt[:, t, :].rearrange("p (h j e) -> p h j e", h=HEADS_PER_BLK, e=2),
                        in0=acc4,
                        in1=ta[:, t : t + 1, :].rearrange("p o (j e) -> p o j e", e=2).to_broadcast(by_head),
                        op=ALU.mult,
                    )
                    nc.vector.tensor_tensor(
                        out=qt[:, t, :].rearrange("p (h j e) -> p h j e", h=HEADS_PER_BLK, e=2),
                        in0=acc4[:, :, :, ::-1],
                        in1=tb[:, t : t + 1, :].rearrange("p o (j e) -> p o j e", e=2).to_broadcast(by_head),
                        op=ALU.mult,
                    )
                    continue
                for h in range(HEADS_PER_BLK):
                    cols = slice(h * HD, (h + 1) * HD)
                    nc.vector.scalar_tensor_tensor(
                        out=pt[:, t, cols],
                        in0=acc[:, cols],
                        scalar=rstd[:, t, h : h + 1],
                        in1=ta[:, t, :],
                        op0=ALU.mult,
                        op1=ALU.mult,
                    )
                    nc.vector.scalar_tensor_tensor(
                        out=qt[:, t, cols].rearrange("p (j e) -> p j e", e=2),
                        in0=acc[:, cols].rearrange("p (j e) -> p j e", e=2)[:, :, ::-1],
                        scalar=rstd[:, t, h : h + 1],
                        in1=tb[:, t, :].rearrange("p (j e) -> p j e", e=2),
                        op0=ALU.mult,
                        op1=ALU.mult,
                    )
                if halves_on is not None and t % 2 == 1:
                    halves_on.tensor_tensor(
                        out=pt[:, t - 1 : t + 1, :].rearrange("p t n -> p (t n)"),
                        in0=pt[:, t - 1 : t + 1, :].rearrange("p t n -> p (t n)"),
                        in1=qt[:, t - 1 : t + 1, :].rearrange("p t n -> p (t n)"),
                        op=ALU.add,
                    )
                    nc.sync.dma_start(out=out_block(c, n)[:, t - 1 : t + 1, :], in_=pt[:, t - 1 : t + 1, :])
            if halves_on is not None:
                return None
            if last:
                for t in range(0, TPG, 2):
                    nc.vector.tensor_tensor(
                        out=pt[:, t : t + 2, :], in0=pt[:, t : t + 2, :], in1=qt[:, t : t + 2, :], op=ALU.add
                    )
                    nc.sync.dma_start(out=out_block(c, n)[:, t : t + 2, :], in_=pt[:, t : t + 2, :])
                return None
            nc.gpsimd.tensor_tensor(
                out=pt[:].rearrange("p t n -> p (t n)"),
                in0=pt[:].rearrange("p t n -> p (t n)"),
                in1=qt[:].rearrange("p t n -> p (t n)"),
                op=ALU.add,
            )
            if wide:
                return (pt, rstd, c, n)
            nc.sync.dma_start(out=out_block(c, n), in_=pt[:])
            return None

        def finish_wide(todo):
            pt, rstd, c, n = todo
            for t in range(TPG):
                for h in range(HEADS_PER_BLK):
                    cols = slice(h * HD, (h + 1) * HD)
                    nc.scalar.activation(
                        out=pt[:, t, cols], in_=pt[:, t, cols], func=ACT.Copy, scale=rstd[:, t, h : h + 1]
                    )
            nc.sync.dma_start(out=out_block(c, n), in_=pt[:])

        v_done = 0
        waiting = []
        finished = 0
        n_blocks = GROUPS * V_BLOCK
        for b in range(n_blocks):
            c = b // V_BLOCK
            n = b % V_BLOCK
            todo = qk_block(c, n, False, False, {n_blocks - 2: nc.gpsimd, n_blocks - 1: nc.vector}.get(b))
            if todo is not None:
                waiting.append(todo)
            if finished < len(waiting) and waiting[finished][2] * V_BLOCK + waiting[finished][3] <= b - 2:
                finish_wide(waiting[finished])
                finished += 1
            if b >= V_FIRST and b % 3 != 2:
                v_bank(v_done)
                v_done += 1
            if b == 1:
                build_tables(nc.gpsimd, 2)
        for i in range(v_done, TOKEN_TILES - 1):
            v_bank(i, queue=nc.scalar)
        for first_col in range(0, NBLK, NBLK // 2):
            v_bank(TOKEN_TILES - 1, first_col, NBLK // 2, queue=nc.scalar)
